import numpy as np
import ml_dtypes

BF16 = ml_dtypes.bfloat16


def bf(x):
    return np.asarray(x, np.float32).astype(BF16)


def f32(x):
    return np.asarray(x, np.float32)


def f64(x):
    return np.asarray(x).astype(np.float64)


def striped(idx):
    return np.tile(idx.reshape(-1, 16).T, (8, 1))


S, D, R, M, N = 1024, 128, 256, 256, 2048
ERF_TERMS, ERF_LIMIT = 150, 6.0


def erf(a):
    a = np.asarray(a, np.float64)
    c = np.clip(a, -ERF_LIMIT, ERF_LIMIT)
    term = c.copy()
    total = c.copy()
    for t in range(1, ERF_TERMS):
        term = term * 2.0 * c * c / (2.0 * t + 1.0)
        total = total + term
    val = 2.0 / np.sqrt(np.pi) * np.exp(-c * c) * total
    return np.where(np.abs(a) > ERF_LIMIT, np.sign(a), val)


def gelu(v):
    return 0.5 * v * (1.0 + erf(v / np.sqrt(2.0)))


def setup_inputs():
    s1 = np.sqrt(2.0 / (D + R + M))
    s2 = np.sqrt(2.0 / (M + M))
    s3 = np.sqrt(2.0 / (M + 1))
    return {
        "table": bf(np.random.standard_normal((D, S))),
        "w": bf(s1 * np.random.standard_normal((D, M))),
        "rest": bf(np.random.standard_normal((R, N))),
        "w_rest": bf(s1 * np.random.standard_normal((R, M))),
        "b1": f32(0.1 * np.random.standard_normal((M, 1))),
        "w2": bf(s2 * np.random.standard_normal((M, M))),
        "b2": f32(0.1 * np.random.standard_normal((M, 1))),
        "w3": bf(s3 * np.random.standard_normal((M, 1))),
        "b3": f32(0.1 + 0.2 * np.random.random((1, 1))),
        "z": f32(np.random.standard_normal((1, N))),
        "offs": striped(np.random.permutation(np.tile(np.arange(S), 2))[:N]),
    }


def reference(table, w, rest, w_rest, b1, w2, b2, w3, b3, z, offs):
    idx = offs[:16].T.reshape(-1)
    h1 = gelu(f64(w).T @ f64(table)[:, idx] + f64(w_rest).T @ f64(rest) + f64(b1))
    h2 = gelu(f64(w2).T @ h1 + f64(b2))
    delta = f64(w3).T @ h2 + f64(b3)
    return np.tanh(f64(z) + delta)

@@ -1,0 +1,111 @@
+import concourse.mybir as mybir
+
+BF16, F32, U16 = mybir.dt.bfloat16, mybir.dt.float32, mybir.dt.uint16
+GELU = mybir.ActivationFunctionType.Gelu
+TANH = mybir.ActivationFunctionType.Tanh
+ADD = mybir.AluOpType.add
+
+P = 128
+S, D, R, M, N = 1024, 128, 256, 256, 2048
+PIECE = 512
+N_PIECES = N // PIECE
+HALVES = M // P
+R_BLOCKS = R // P
+QUAD = P // N_PIECES
+LIST_COLS = PIECE // 16
+BANKS = 8
+
+FLOPS = 2 * N * (D * M + R * M + M * M + M)
+
+
+def tile_expertpredictionheads_kernel(tc, table, w, rest, w_rest, b1, w2, b2, w3, b3, z, offs, out):
+    nc = tc.nc
+    with (
+        tc.tile_pool(name="held", bufs=1) as held,
+        tc.tile_pool(name="pieces", bufs=N_PIECES) as pieces,
+        tc.psum_pool(name="psum", bufs=BANKS) as psum,
+    ):
+        offsets = held.tile([P, N // 16], U16, name="offsets")
+        nc.sync.dma_start(offsets[:], offs)
+        w_sb = held.tile([P, M], BF16, name="w_sb")
+        nc.scalar.dma_start(w_sb[:], w)
+        table_sb = held.tile([P, S], BF16, name="table_sb")
+        nc.sync.dma_start(table_sb[:], table)
+
+        rest_blocks = rest.rearrange("(k p) n -> p k n", p=P)
+        rest_sb = [pieces.tile([P, R_BLOCKS, PIECE], BF16, name="rest_sb") for c in range(N_PIECES)]
+        for c in range(N_PIECES):
+            nc.sync.dma_start(rest_sb[c][:], rest_blocks[:, :, c * PIECE : (c + 1) * PIECE])
+
+        w_rest_sb = held.tile([P, R_BLOCKS, M], BF16, name="w_rest_sb")
+        nc.scalar.dma_start(w_rest_sb[:], w_rest.rearrange("(k p) m -> p k m", p=P))
+        b1_sb = held.tile([P, HALVES], F32, name="b1_sb")
+        b2_sb = held.tile([P, HALVES], F32, name="b2_sb")
+        w3_sb = held.tile([P, HALVES], BF16, name="w3_sb")
+        w2_sb = held.tile([P, HALVES, M], BF16, name="w2_sb")
+        with nc.allow_non_contiguous_dma(reason="256 single elements, one to a partition and half"):
+            nc.scalar.dma_start(b1_sb[:], b1.rearrange("(h p) o -> p (h o)", p=P))
+            nc.scalar.dma_start(w2_sb[:], w2.rearrange("(k p) m -> p k m", p=P))
+            nc.scalar.dma_start(b2_sb[:], b2.rearrange("(h p) o -> p (h o)", p=P))
+            nc.scalar.dma_start(w3_sb[:], w3.rearrange("(h p) o -> p (h o)", p=P))
+        b3_sb = held.tile([P, 1], F32, name="b3_sb")
+        nc.scalar.dma_start(b3_sb[:], b3.to_broadcast([P, 1]))
+        z_sb = held.tile([P, PIECE], F32, name="z_sb")
+        for c in range(N_PIECES):
+            nc.scalar.dma_start(
+                z_sb[c * QUAD : (c + 1) * QUAD, :], z[0:1, c * PIECE : (c + 1) * PIECE].to_broadcast([QUAD, PIECE])
+            )
+
+        w3_cols = held.tile([P, HALVES, QUAD], BF16, name="w3_cols")
+        nc.vector.tensor_copy(w3_cols[:], w3_sb[:].unsqueeze(2).to_broadcast([P, HALVES, QUAD]))
+
+        h1 = [pieces.tile([P, HALVES, PIECE], BF16, name="h1") for c in range(N_PIECES)]
+        h2 = [pieces.tile([P, HALVES, PIECE], BF16, name="h2") for c in range(N_PIECES)]
+
+        sum1 = {}
+        for c in range(N_PIECES):
+            picked = table_sb[:].indirect(offsets[:, c * LIST_COLS : (c + 1) * LIST_COLS])
+            for h in range(HALVES):
+                sum1[c, h] = psum.tile([P, PIECE], F32, name="sum1", tag="bank")
+                nc.tensor.matmul(sum1[c, h][:], w_sb[:, h * P : (h + 1) * P], picked, start=True, stop=False)
+
+        def finish_layer1(c):
+            for h in range(HALVES):
+                for k in range(R_BLOCKS):
+                    nc.tensor.matmul(
+                        sum1[c, h][:], w_rest_sb[:, k, h * P : (h + 1) * P], rest_sb[c][:, k, :],
+                        start=False, stop=(k == R_BLOCKS - 1),
+                    )
+                nc.scalar.activation(h1[c][:, h, :], sum1[c, h][:], GELU, bias=b1_sb[:, h : h + 1])
+
+        def layer2(c):
+            for h in range(HALVES):
+                sum2 = psum.tile([P, PIECE], F32, name="sum2", tag="bank")
+                for k in range(HALVES):
+                    nc.tensor.matmul(
+                        sum2[:], w2_sb[:, k, h * P : (h + 1) * P], h1[c][:, k, :],
+                        start=(k == 0), stop=(k == HALVES - 1),
+                    )
+                nc.scalar.activation(h2[c][:, h, :], sum2[:], GELU, bias=b2_sb[:, h : h + 1])
+
+        finish_layer1(0)
+        for c in range(1, N_PIECES):
+            finish_layer1(c)
+            layer2(c - 1)
+        layer2(N_PIECES - 1)
+
+        sum3 = psum.tile([P, PIECE], F32, name="sum3", tag="bank")
+        for c in range(N_PIECES):
+            for k in range(HALVES):
+                nc.tensor.matmul(
+                    sum3[c * QUAD : (c + 1) * QUAD, :], w3_cols[:, k, :], h2[c][:, k, :],
+                    start=(k == 0), stop=(k == HALVES - 1),
+                )
+
+        with_z = held.tile([P, PIECE], F32, name="with_z")
+        nc.vector.tensor_tensor(with_z[:], sum3[:], z_sb[:], ADD)
+        squashed = held.tile([P, PIECE], F32, name="squashed")
+        nc.scalar.activation(squashed[:], with_z[:], TANH, bias=b3_sb[:])
+
+        first_rows = squashed[:].rearrange("(c r) n -> c r n", r=QUAD)[:, 0, :]
+        nc.sync.dma_start(out.rearrange("o (c n) -> (o c) n", c=N_PIECES), first_rows)

@@ -9,6 +9,8 @@ P = 128
 S, D, R, M, N = 1024, 128, 256, 256, 2048
 PIECE = 512
 N_PIECES = N // PIECE
+EARLY = (0, 1)
+LATE = (2, 3)
 HALVES = M // P
 R_BLOCKS = R // P
 QUAD = P // N_PIECES
@@ -27,32 +29,38 @@ def tile_expertpredictionheads_kernel(tc, table, w, rest, w_rest, b1, w2, b2, w3
     ):
         offsets = held.tile([P, N // 16], U16, name="offsets")
         nc.sync.dma_start(offsets[:], offs)
-        w_sb = held.tile([P, M], BF16, name="w_sb")
-        nc.scalar.dma_start(w_sb[:], w)
         table_sb = held.tile([P, S], BF16, name="table_sb")
         nc.sync.dma_start(table_sb[:], table)
+        w_sb = held.tile([P, M], BF16, name="w_sb")
+        nc.sync.dma_start(w_sb[:], w)
 
-        rest_blocks = rest.rearrange("(k p) n -> p k n", p=P)
-        rest_sb = [pieces.tile([P, R_BLOCKS, PIECE], BF16, name="rest_sb") for c in range(N_PIECES)]
-        for c in range(N_PIECES):
-            nc.sync.dma_start(rest_sb[c][:], rest_blocks[:, :, c * PIECE : (c + 1) * PIECE])
-
-        w_rest_sb = held.tile([P, R_BLOCKS, M], BF16, name="w_rest_sb")
-        nc.scalar.dma_start(w_rest_sb[:], w_rest.rearrange("(k p) m -> p k m", p=P))
         b1_sb = held.tile([P, HALVES], F32, name="b1_sb")
         b2_sb = held.tile([P, HALVES], F32, name="b2_sb")
         w3_sb = held.tile([P, HALVES], BF16, name="w3_sb")
+        w_rest_sb = held.tile([P, R_BLOCKS, M], BF16, name="w_rest_sb")
         w2_sb = held.tile([P, HALVES, M], BF16, name="w2_sb")
-        with nc.allow_non_contiguous_dma(reason="256 single elements, one to a partition and half"):
-            nc.scalar.dma_start(b1_sb[:], b1.rearrange("(h p) o -> p (h o)", p=P))
-            nc.scalar.dma_start(w2_sb[:], w2.rearrange("(k p) m -> p k m", p=P))
-            nc.scalar.dma_start(b2_sb[:], b2.rearrange("(h p) o -> p (h o)", p=P))
-            nc.scalar.dma_start(w3_sb[:], w3.rearrange("(h p) o -> p (h o)", p=P))
+        rest_early = held.tile([P, R_BLOCKS, len(EARLY) * PIECE], BF16, name="rest_early")
+        rest_late = held.tile([P, R_BLOCKS, len(LATE) * PIECE], BF16, name="rest_late")
+        rest_blocks = rest.rearrange("(k p) n -> p k n", p=P)
+        with nc.allow_non_contiguous_dma(reason="b1, b2, w3: 256 single elements, one to a partition and half"):
+            nc.sync.dma_start(b1_sb[:], b1.rearrange("(h p) o -> p (h o)", p=P))
+            nc.sync.dma_start(w_rest_sb[:], w_rest.rearrange("(k p) m -> p k m", p=P))
+            nc.sync.dma_start(rest_early[:], rest_blocks[:, :, 0 : LATE[0] * PIECE])
+            nc.sync.dma_start(w2_sb[:], w2.rearrange("(k p) m -> p k m", p=P))
+            nc.sync.dma_start(b2_sb[:], b2.rearrange("(h p) o -> p (h o)", p=P))
+            nc.sync.dma_start(rest_late[:], rest_blocks[:, :, LATE[0] * PIECE : N])
+            nc.sync.dma_start(w3_sb[:], w3.rearrange("(h p) o -> p (h o)", p=P))
+
+        def rest_of(c, k):
+            if c in EARLY:
+                return rest_early[:, k, c * PIECE : (c + 1) * PIECE]
+            return rest_late[:, k, (c - LATE[0]) * PIECE : (c - LATE[0] + 1) * PIECE]
+
         b3_sb = held.tile([P, 1], F32, name="b3_sb")
-        nc.scalar.dma_start(b3_sb[:], b3.to_broadcast([P, 1]))
+        nc.gpsimd.dma_start(b3_sb[:], b3.to_broadcast([P, 1]))
         z_sb = held.tile([P, PIECE], F32, name="z_sb")
         for c in range(N_PIECES):
-            nc.scalar.dma_start(
+            nc.gpsimd.dma_start(
                 z_sb[c * QUAD : (c + 1) * QUAD, :], z[0:1, c * PIECE : (c + 1) * PIECE].to_broadcast([QUAD, PIECE])
             )
 
@@ -61,22 +69,21 @@ def tile_expertpredictionheads_kernel(tc, table, w, rest, w_rest, b1, w2, b2, w3
 
         h1 = [pieces.tile([P, HALVES, PIECE], BF16, name="h1") for c in range(N_PIECES)]
         h2 = [pieces.tile([P, HALVES, PIECE], BF16, name="h2") for c in range(N_PIECES)]
-
         sum1 = {}
-        for c in range(N_PIECES):
-            picked = table_sb[:].indirect(offsets[:, c * LIST_COLS : (c + 1) * LIST_COLS])
-            for h in range(HALVES):
-                sum1[c, h] = psum.tile([P, PIECE], F32, name="sum1", tag="bank")
-                nc.tensor.matmul(sum1[c, h][:], w_sb[:, h * P : (h + 1) * P], picked, start=True, stop=False)
 
-        def finish_layer1(c):
-            for h in range(HALVES):
-                for k in range(R_BLOCKS):
-                    nc.tensor.matmul(
-                        sum1[c, h][:], w_rest_sb[:, k, h * P : (h + 1) * P], rest_sb[c][:, k, :],
-                        start=False, stop=(k == R_BLOCKS - 1),
-                    )
-                nc.scalar.activation(h1[c][:, h, :], sum1[c, h][:], GELU, bias=b1_sb[:, h : h + 1])
+        def look_up(c, h, opens):
+            picked = table_sb[:].indirect(offsets[:, c * LIST_COLS : (c + 1) * LIST_COLS])
+            nc.tensor.matmul(sum1[c, h][:], w_sb[:, h * P : (h + 1) * P], picked, start=opens, stop=not opens)
+
+        def add_rest(c, h, opens):
+            for k in range(R_BLOCKS):
+                nc.tensor.matmul(
+                    sum1[c, h][:], w_rest_sb[:, k, h * P : (h + 1) * P], rest_of(c, k),
+                    start=(opens and k == 0), stop=(not opens and k == R_BLOCKS - 1),
+                )
+
+        def gelu1(c, h):
+            nc.scalar.activation(h1[c][:, h, :], sum1[c, h][:], GELU, bias=b1_sb[:, h : h + 1])
 
         def layer2(c):
             for h in range(HALVES):
@@ -88,11 +95,26 @@ def tile_expertpredictionheads_kernel(tc, table, w, rest, w_rest, b1, w2, b2, w3
                     )
                 nc.scalar.activation(h2[c][:, h, :], sum2[:], GELU, bias=b2_sb[:, h : h + 1])
 
-        finish_layer1(0)
-        for c in range(1, N_PIECES):
-            finish_layer1(c)
-            layer2(c - 1)
-        layer2(N_PIECES - 1)
+        for c in EARLY:
+            for h in range(HALVES):
+                sum1[c, h] = psum.tile([P, PIECE], F32, name="sum1", tag="bank")
+                look_up(c, h, opens=True)
+        for c in EARLY:
+            for h in range(HALVES):
+                add_rest(c, h, opens=False)
+                gelu1(c, h)
+        for c in EARLY:
+            layer2(c)
+        for c in LATE:
+            for h in range(HALVES):
+                sum1[c, h] = psum.tile([P, PIECE], F32, name="sum1", tag="bank")
+                add_rest(c, h, opens=True)
+        for c in LATE:
+            for h in range(HALVES):
+                look_up(c, h, opens=False)
+                gelu1(c, h)
+        for c in LATE:
+            layer2(c)
 
         sum3 = psum.tile([P, PIECE], F32, name="sum3", tag="bank")
         for c in range(N_PIECES):

@@ -13,7 +13,9 @@ EARLY = (0, 1)
 LATE = (2, 3)
 HALVES = M // P
 R_BLOCKS = R // P
-QUAD = P // N_PIECES
+QUAD = 32
+QUARTERS = P // QUAD
+QUARTER = PIECE // QUARTERS
 LIST_COLS = PIECE // 16
 BANKS = 8
 
@@ -58,10 +60,11 @@ def tile_expertpredictionheads_kernel(tc, table, w, rest, w_rest, b1, w2, b2, w3
 
         b3_sb = held.tile([P, 1], F32, name="b3_sb")
         nc.gpsimd.dma_start(b3_sb[:], b3.to_broadcast([P, 1]))
-        z_sb = held.tile([P, PIECE], F32, name="z_sb")
-        for c in range(N_PIECES):
+        z_sb = held.tile([P, N_PIECES, QUARTER], F32, name="z_sb")
+        z_quarters = z.rearrange("o (c q i) -> o c q i", c=N_PIECES, q=QUARTERS)
+        for q in range(QUARTERS):
             nc.gpsimd.dma_start(
-                z_sb[c * QUAD : (c + 1) * QUAD, :], z[0:1, c * PIECE : (c + 1) * PIECE].to_broadcast([QUAD, PIECE])
+                z_sb[q * QUAD : (q + 1) * QUAD, :, :], z_quarters[:, :, q, :].to_broadcast([QUAD, N_PIECES, QUARTER])
             )
 
         w3_cols = held.tile([P, HALVES, QUAD], BF16, name="w3_cols")
@@ -69,6 +72,7 @@ def tile_expertpredictionheads_kernel(tc, table, w, rest, w_rest, b1, w2, b2, w3
 
         h1 = [pieces.tile([P, HALVES, PIECE], BF16, name="h1") for c in range(N_PIECES)]
         h2 = [pieces.tile([P, HALVES, PIECE], BF16, name="h2") for c in range(N_PIECES)]
+        squashed = held.tile([P, N_PIECES, QUARTER], F32, name="squashed")
         sum1 = {}
 
         def look_up(c, h, opens):
@@ -95,6 +99,18 @@ def tile_expertpredictionheads_kernel(tc, table, w, rest, w_rest, b1, w2, b2, w3
                     )
                 nc.scalar.activation(h2[c][:, h, :], sum2[:], GELU, bias=b2_sb[:, h : h + 1])
 
+        def layer3(c):
+            sum3 = psum.tile([P, QUARTER], F32, name="sum3", tag="bank")
+            for q in range(QUARTERS):
+                for k in range(HALVES):
+                    nc.tensor.matmul(
+                        sum3[q * QUAD : (q + 1) * QUAD, :], w3_cols[:, k, :], h2[c][:, k, q * QUARTER : (q + 1) * QUARTER],
+                        start=(k == 0), stop=(k == HALVES - 1),
+                    )
+            with_z = pieces.tile([P, QUARTER], F32, name="with_z")
+            nc.vector.tensor_tensor(with_z[:], sum3[:], z_sb[:, c, :], ADD)
+            nc.scalar.activation(squashed[:, c, :], with_z[:], TANH, bias=b3_sb[:])
+
         for c in EARLY:
             for h in range(HALVES):
                 sum1[c, h] = psum.tile([P, PIECE], F32, name="sum1", tag="bank")
@@ -113,21 +129,12 @@ def tile_expertpredictionheads_kernel(tc, table, w, rest, w_rest, b1, w2, b2, w3
             for h in range(HALVES):
                 look_up(c, h, opens=False)
                 gelu1(c, h)
+        layer3(EARLY[0])
+        layer2(LATE[0])
+        layer3(EARLY[1])
+        layer2(LATE[1])
         for c in LATE:
-            layer2(c)
+            layer3(c)
 
-        sum3 = psum.tile([P, PIECE], F32, name="sum3", tag="bank")
-        for c in range(N_PIECES):
-            for k in range(HALVES):
-                nc.tensor.matmul(
-                    sum3[c * QUAD : (c + 1) * QUAD, :], w3_cols[:, k, :], h2[c][:, k, :],
-                    start=(k == 0), stop=(k == HALVES - 1),
-                )
-
-        with_z = held.tile([P, PIECE], F32, name="with_z")
-        nc.vector.tensor_tensor(with_z[:], sum3[:], z_sb[:], ADD)
-        squashed = held.tile([P, PIECE], F32, name="squashed")
-        nc.scalar.activation(squashed[:], with_z[:], TANH, bias=b3_sb[:])
-
-        first_rows = squashed[:].rearrange("(c r) n -> c r n", r=QUAD)[:, 0, :]
-        nc.sync.dma_start(out.rearrange("o (c n) -> (o c) n", c=N_PIECES), first_rows)
+        first_rows = squashed[:].rearrange("(q r) c i -> q r c i", r=QUAD)[:, 0, :, :]
+        nc.sync.dma_start(out.rearrange("o (c q i) -> q (o c) i", c=N_PIECES, q=QUARTERS), first_rows)

@@ -129,11 +129,9 @@ def tile_expertpredictionheads_kernel(tc, table, w, rest, w_rest, b1, w2, b2, w3
             for h in range(HALVES):
                 look_up(c, h, opens=False)
                 gelu1(c, h)
-        layer3(EARLY[0])
-        layer2(LATE[0])
-        layer3(EARLY[1])
-        layer2(LATE[1])
         for c in LATE:
+            layer2(c)
+        for c in range(N_PIECES):
             layer3(c)
 
         first_rows = squashed[:].rearrange("(q r) c i -> q r c i", r=QUAD)[:, 0, :, :]

@@ -59,13 +59,16 @@ def tile_expertpredictionheads_kernel(tc, table, w, rest, w_rest, b1, w2, b2, w3
             return rest_late[:, k, (c - LATE[0]) * PIECE : (c - LATE[0] + 1) * PIECE]
 
         b3_sb = held.tile([P, 1], F32, name="b3_sb")
-        nc.gpsimd.dma_start(b3_sb[:], b3.to_broadcast([P, 1]))
+        nc.sync.dma_start(b3_sb[:], b3.to_broadcast([P, 1]))
+        def first_rows(tile):
+            return tile[:].rearrange("(q r) c i -> q r c i", r=QUAD)[:, 0, :, :]
+
+        def in_quarters(row):
+            return row.rearrange("o (c q i) -> q (o c) i", c=N_PIECES, q=QUARTERS)
+
         z_sb = held.tile([P, N_PIECES, QUARTER], F32, name="z_sb")
-        z_quarters = z.rearrange("o (c q i) -> o c q i", c=N_PIECES, q=QUARTERS)
-        for q in range(QUARTERS):
-            nc.gpsimd.dma_start(
-                z_sb[q * QUAD : (q + 1) * QUAD, :, :], z_quarters[:, :, q, :].to_broadcast([QUAD, N_PIECES, QUARTER])
-            )
+        nc.vector.memset(z_sb[:], 0.0)
+        nc.sync.dma_start(first_rows(z_sb), in_quarters(z))
 
         w3_cols = held.tile([P, HALVES, QUAD], BF16, name="w3_cols")
         nc.vector.tensor_copy(w3_cols[:], w3_sb[:].unsqueeze(2).to_broadcast([P, HALVES, QUAD]))
@@ -134,5 +137,4 @@ def tile_expertpredictionheads_kernel(tc, table, w, rest, w_rest, b1, w2, b2, w3
         for c in range(N_PIECES):
             layer3(c)
 
-        first_rows = squashed[:].rearrange("(q r) c i -> q r c i", r=QUAD)[:, 0, :, :]
-        nc.sync.dma_start(out.rearrange("o (c q i) -> q (o c) i", c=N_PIECES, q=QUARTERS), first_rows)
+        nc.sync.dma_start(in_quarters(out), first_rows(squashed))

@@ -41,22 +41,22 @@ def tile_expertpredictionheads_kernel(tc, table, w, rest, w_rest, b1, w2, b2, w3
         w3_sb = held.tile([P, HALVES], BF16, name="w3_sb")
         w_rest_sb = held.tile([P, R_BLOCKS, M], BF16, name="w_rest_sb")
         w2_sb = held.tile([P, HALVES, M], BF16, name="w2_sb")
-        rest_early = held.tile([P, R_BLOCKS, len(EARLY) * PIECE], BF16, name="rest_early")
-        rest_late = held.tile([P, R_BLOCKS, len(LATE) * PIECE], BF16, name="rest_late")
+        rest_sb = [held.tile([P, R_BLOCKS, PIECE], BF16, name="rest_sb%d" % c) for c in range(N_PIECES)]
         rest_blocks = rest.rearrange("(k p) n -> p k n", p=P)
+
+        def load_rest(c):
+            nc.sync.dma_start(rest_sb[c][:], rest_blocks[:, :, c * PIECE : (c + 1) * PIECE])
+
         with nc.allow_non_contiguous_dma(reason="b1, b2, w3: 256 single elements, one to a partition and half"):
-            nc.sync.dma_start(b1_sb[:], b1.rearrange("(h p) o -> p (h o)", p=P))
             nc.sync.dma_start(w_rest_sb[:], w_rest.rearrange("(k p) m -> p k m", p=P))
-            nc.sync.dma_start(rest_early[:], rest_blocks[:, :, 0 : LATE[0] * PIECE])
+            load_rest(0)
+            nc.sync.dma_start(b1_sb[:], b1.rearrange("(h p) o -> p (h o)", p=P))
+            load_rest(1)
             nc.sync.dma_start(w2_sb[:], w2.rearrange("(k p) m -> p k m", p=P))
             nc.sync.dma_start(b2_sb[:], b2.rearrange("(h p) o -> p (h o)", p=P))
-            nc.sync.dma_start(rest_late[:], rest_blocks[:, :, LATE[0] * PIECE : N])
+            load_rest(2)
+            load_rest(3)
             nc.sync.dma_start(w3_sb[:], w3.rearrange("(h p) o -> p (h o)", p=P))
-
-        def rest_of(c, k):
-            if c in EARLY:
-                return rest_early[:, k, c * PIECE : (c + 1) * PIECE]
-            return rest_late[:, k, (c - LATE[0]) * PIECE : (c - LATE[0] + 1) * PIECE]
 
         b3_sb = held.tile([P, 1], F32, name="b3_sb")
         nc.sync.dma_start(b3_sb[:], b3.to_broadcast([P, 1]))
@@ -85,7 +85,7 @@ def tile_expertpredictionheads_kernel(tc, table, w, rest, w_rest, b1, w2, b2, w3
         def add_rest(c, h, opens):
             for k in range(R_BLOCKS):
                 nc.tensor.matmul(
-                    sum1[c, h][:], w_rest_sb[:, k, h * P : (h + 1) * P], rest_of(c, k),
+                    sum1[c, h][:], w_rest_sb[:, k, h * P : (h + 1) * P], rest_sb[c][:, k, :],
                     start=(opens and k == 0), stop=(not opens and k == R_BLOCKS - 1),
                 )
 

@@ -113,6 +113,7 @@ def tile_expertpredictionheads_kernel(tc, table, w, rest, w_rest, b1, w2, b2, w3
             with_z = pieces.tile([P, QUARTER], F32, name="with_z")
             nc.vector.tensor_tensor(with_z[:], sum3[:], z_sb[:, c, :], ADD)
             nc.scalar.activation(squashed[:, c, :], with_z[:], TANH, bias=b3_sb[:])
+            nc.sync.dma_start(in_quarters(out)[:, c, :], first_rows(squashed)[:, c, :])
 
         for c in EARLY:
             for h in range(HALVES):
@@ -136,5 +137,3 @@ def tile_expertpredictionheads_kernel(tc, table, w, rest, w_rest, b1, w2, b2, w3
             layer2(c)
         for c in range(N_PIECES):
             layer3(c)
-
-        nc.sync.dma_start(in_quarters(out), first_rows(squashed))

@@ -1,9 +1,11 @@
 import concourse.mybir as mybir
+from concourse.masks import make_identity
 
 BF16, F32, U16 = mybir.dt.bfloat16, mybir.dt.float32, mybir.dt.uint16
 GELU = mybir.ActivationFunctionType.Gelu
 TANH = mybir.ActivationFunctionType.Tanh
-ADD = mybir.AluOpType.add
+ADD, SUBTRACT = mybir.AluOpType.add, mybir.AluOpType.subtract
+MIN, MAX = mybir.AluOpType.min, mybir.AluOpType.max
 
 P = 128
 S, D, R, M, N = 1024, 128, 256, 256, 2048
@@ -17,6 +19,9 @@ QUAD = 32
 QUARTERS = P // QUAD
 QUARTER = PIECE // QUARTERS
 LIST_COLS = PIECE // 16
+Z_LIMIT = 3.0e38
+TERM_ROWS = (0, 64, 96)
+L3_GROUPS = ((0, 1, 2), (3,))
 BANKS = 8
 
 FLOPS = 2 * N * (D * M + R * M + M * M + M)
@@ -60,22 +65,36 @@ def tile_expertpredictionheads_kernel(tc, table, w, rest, w_rest, b1, w2, b2, w3
 
         b3_sb = held.tile([P, 1], F32, name="b3_sb")
         nc.sync.dma_start(b3_sb[:], b3.to_broadcast([P, 1]))
-        def first_rows(tile):
-            return tile[:].rearrange("(q r) c i -> q r c i", r=QUAD)[:, 0, :, :]
-
         def in_quarters(row):
             return row.rearrange("o (c q i) -> q (o c) i", c=N_PIECES, q=QUARTERS)
 
-        z_sb = held.tile([P, N_PIECES, QUARTER], F32, name="z_sb")
-        nc.vector.memset(z_sb[:], 0.0)
-        nc.sync.dma_start(first_rows(z_sb), in_quarters(z))
+        z_copies = held.tile([P, N_PIECES, QUARTER], F32, name="z_copies")
+        nc.vector.memset(z_copies[:], 0.0)
+        for first in TERM_ROWS:
+            nc.sync.dma_start(z_copies[first : first + QUARTERS], in_quarters(z))
+        nc.vector.tensor_scalar(z_copies[:], z_copies[:], Z_LIMIT, -Z_LIMIT, MIN, MAX)
+        z_terms = held.tile([P, N_PIECES, QUARTER], BF16, name="z_terms")
+        nc.vector.tensor_copy(z_terms[:], z_copies[:])
+        for first in TERM_ROWS[1:]:
+            left = held.tile([P, N_PIECES, QUARTER], F32, name="left%d" % first)
+            nc.vector.tensor_tensor(left[first:], z_copies[first:], z_terms[first:], SUBTRACT)
+            nc.vector.tensor_copy(z_terms[first:], left[first:])
+            z_copies = left
+        identity = held.tile([P, P], BF16, name="identity")
+        make_identity(nc, identity[:])
+        two_terms = held.tile([P, QUARTERS], BF16, name="two_terms")
+        three_terms = held.tile([P, QUARTERS], BF16, name="three_terms")
+        hi, mid, lo = [identity[:, first : first + QUARTERS] for first in TERM_ROWS]
+        nc.vector.tensor_tensor(two_terms[:], hi, mid, ADD)
+        nc.vector.tensor_tensor(three_terms[:], two_terms[:], lo, ADD)
+        sum_terms = held.tile([P, QUARTERS, QUAD], BF16, name="sum_terms")
+        nc.vector.tensor_copy(sum_terms[:], three_terms[:].unsqueeze(2).to_broadcast([P, QUARTERS, QUAD]))
 
         w3_cols = held.tile([P, HALVES, QUAD], BF16, name="w3_cols")
         nc.vector.tensor_copy(w3_cols[:], w3_sb[:].unsqueeze(2).to_broadcast([P, HALVES, QUAD]))
 
         h1 = [pieces.tile([P, HALVES, PIECE], BF16, name="h1") for c in range(N_PIECES)]
         h2 = [pieces.tile([P, HALVES, PIECE], BF16, name="h2") for c in range(N_PIECES)]
-        squashed = held.tile([P, N_PIECES, QUARTER], F32, name="squashed")
         sum1 = {}
 
         def look_up(c, h, opens):
@@ -102,18 +121,21 @@ def tile_expertpredictionheads_kernel(tc, table, w, rest, w_rest, b1, w2, b2, w3
                     )
                 nc.scalar.activation(h2[c][:, h, :], sum2[:], GELU, bias=b2_sb[:, h : h + 1])
 
-        def layer3(c):
-            sum3 = psum.tile([P, QUARTER], F32, name="sum3", tag="bank")
-            for q in range(QUARTERS):
+        def layer3(group):
+            sum3 = psum.tile([P, len(group), QUARTER], F32, name="sum3", tag="bank")
+            nc.tensor.matmul(sum3[:], sum_terms[:], z_terms[:, group[0] : group[-1] + 1, :], start=True, stop=False)
+            for slot, c in enumerate(group):
                 for k in range(HALVES):
-                    nc.tensor.matmul(
-                        sum3[q * QUAD : (q + 1) * QUAD, :], w3_cols[:, k, :], h2[c][:, k, q * QUARTER : (q + 1) * QUARTER],
-                        start=(k == 0), stop=(k == HALVES - 1),
-                    )
-            with_z = pieces.tile([P, QUARTER], F32, name="with_z")
-            nc.vector.tensor_tensor(with_z[:], sum3[:], z_sb[:, c, :], ADD)
-            nc.scalar.activation(squashed[:, c, :], with_z[:], TANH, bias=b3_sb[:])
-            nc.sync.dma_start(in_quarters(out)[:, c, :], first_rows(squashed)[:, c, :])
+                    for q in range(QUARTERS):
+                        nc.tensor.matmul(
+                            sum3[q * QUAD : (q + 1) * QUAD, slot, :],
+                            w3_cols[:, k, :], h2[c][:, k, q * QUARTER : (q + 1) * QUARTER],
+                            start=False, stop=(c == group[-1] and k == HALVES - 1),
+                        )
+            squashed = held.tile([P, len(group), QUARTER], F32, name="squashed%d" % group[0])
+            nc.scalar.activation(squashed[:], sum3[:], TANH, bias=b3_sb[:])
+            first_rows = squashed[:].rearrange("(q r) c i -> q r c i", r=QUAD)[:, 0, :, :]
+            nc.sync.dma_start(in_quarters(out)[:, group[0] : group[-1] + 1, :], first_rows)
 
         for c in EARLY:
             for h in range(HALVES):
@@ -135,5 +157,5 @@ def tile_expertpredictionheads_kernel(tc, table, w, rest, w_rest, b1, w2, b2, w3
                 gelu1(c, h)
         for c in LATE:
             layer2(c)
-        for c in range(N_PIECES):
-            layer3(c)
+        for group in L3_GROUPS:
+            layer3(group)

@@ -11,17 +11,19 @@ P = 128
 S, D, R, M, N = 1024, 128, 256, 256, 2048
 PIECE = 512
 N_PIECES = N // PIECE
-EARLY = (0, 1)
-LATE = (2, 3)
+WHOLE = (0, 1, 2)
+PART = PIECE // 2
+LAST = N_PIECES - 1
+CHUNKS = [(c, 0, PIECE) for c in WHOLE] + [(LAST, 0, PART), (LAST, PART, PIECE)]
+PART_A, PART_B = len(WHOLE), len(WHOLE) + 1
 HALVES = M // P
 R_BLOCKS = R // P
 QUAD = 32
 QUARTERS = P // QUAD
 QUARTER = PIECE // QUARTERS
-LIST_COLS = PIECE // 16
+LIST_ROWS = 16
 Z_LIMIT = 3.0e38
 TERM_ROWS = (0, 64, 96)
-L3_GROUPS = ((0, 1, 2), (3,))
 BANKS = 8
 
 FLOPS = 2 * N * (D * M + R * M + M * M + M)
@@ -94,68 +96,92 @@ def tile_expertpredictionheads_kernel(tc, table, w, rest, w_rest, b1, w2, b2, w3
         nc.vector.tensor_copy(w3_cols[:], w3_sb[:].unsqueeze(2).to_broadcast([P, HALVES, QUAD]))
 
         h1 = [pieces.tile([P, HALVES, PIECE], BF16, name="h1") for c in range(N_PIECES)]
-        h2 = [pieces.tile([P, HALVES, PIECE], BF16, name="h2") for c in range(N_PIECES)]
+        h2_whole = held.tile([P, HALVES, len(WHOLE), PIECE], BF16, name="h2_whole")
+        h2_last = held.tile([P, HALVES, 1, PIECE], BF16, name="h2_last")
         sum1 = {}
 
-        def look_up(c, h, opens):
-            picked = table_sb[:].indirect(offsets[:, c * LIST_COLS : (c + 1) * LIST_COLS])
-            nc.tensor.matmul(sum1[c, h][:], w_sb[:, h * P : (h + 1) * P], picked, start=opens, stop=not opens)
+        def look_up(chunk, h, opens):
+            c, a, b = CHUNKS[chunk]
+            first, last = (c * PIECE + a) // LIST_ROWS, (c * PIECE + b) // LIST_ROWS
+            picked = table_sb[:].indirect(offsets[:, first:last])
+            nc.tensor.matmul(sum1[chunk, h][:, : b - a], w_sb[:, h * P : (h + 1) * P], picked, start=opens, stop=not opens)
 
-        def add_rest(c, h, opens):
+        def add_rest(chunk, h, opens):
+            c, a, b = CHUNKS[chunk]
             for k in range(R_BLOCKS):
                 nc.tensor.matmul(
-                    sum1[c, h][:], w_rest_sb[:, k, h * P : (h + 1) * P], rest_sb[c][:, k, :],
+                    sum1[chunk, h][:, : b - a], w_rest_sb[:, k, h * P : (h + 1) * P], rest_sb[c][:, k, a:b],
                     start=(opens and k == 0), stop=(not opens and k == R_BLOCKS - 1),
                 )
 
-        def gelu1(c, h):
-            nc.scalar.activation(h1[c][:, h, :], sum1[c, h][:], GELU, bias=b1_sb[:, h : h + 1])
+        def gelu1(chunk, h):
+            c, a, b = CHUNKS[chunk]
+            nc.scalar.activation(h1[c][:, h, a:b], sum1[chunk, h][:, : b - a], GELU, bias=b1_sb[:, h : h + 1])
 
-        def layer2(c):
+        def layer2(chunk):
+            c, a, b = CHUNKS[chunk]
             for h in range(HALVES):
                 sum2 = psum.tile([P, PIECE], F32, name="sum2", tag="bank")
                 for k in range(HALVES):
                     nc.tensor.matmul(
-                        sum2[:], w2_sb[:, k, h * P : (h + 1) * P], h1[c][:, k, :],
+                        sum2[:, : b - a], w2_sb[:, k, h * P : (h + 1) * P], h1[c][:, k, a:b],
                         start=(k == 0), stop=(k == HALVES - 1),
                     )
-                nc.scalar.activation(h2[c][:, h, :], sum2[:], GELU, bias=b2_sb[:, h : h + 1])
+                h2, slot = (h2_last, 0) if c == LAST else (h2_whole, c)
+                nc.scalar.activation(h2[:, h, slot, a:b], sum2[:, : b - a], GELU, bias=b2_sb[:, h : h + 1])
 
-        def layer3(group):
+        def open_with_z(group):
             sum3 = psum.tile([P, len(group), QUARTER], F32, name="sum3", tag="bank")
             nc.tensor.matmul(sum3[:], sum_terms[:], z_terms[:, group[0] : group[-1] + 1, :], start=True, stop=False)
-            for slot, c in enumerate(group):
-                for k in range(HALVES):
-                    for q in range(QUARTERS):
-                        nc.tensor.matmul(
-                            sum3[q * QUAD : (q + 1) * QUAD, slot, :],
-                            w3_cols[:, k, :], h2[c][:, k, q * QUARTER : (q + 1) * QUARTER],
-                            start=False, stop=(c == group[-1] and k == HALVES - 1),
-                        )
+            return sum3
+
+        def add_w3(sum3, h2, k, quarters):
+            for q in quarters:
+                nc.tensor.matmul(
+                    sum3[q * QUAD : (q + 1) * QUAD], w3_cols[:, k, :], h2[:, k, :, q * QUARTER : (q + 1) * QUARTER],
+                    start=False, stop=(k == HALVES - 1),
+                )
+
+        def squash_and_store(sum3, group):
             squashed = held.tile([P, len(group), QUARTER], F32, name="squashed%d" % group[0])
             nc.scalar.activation(squashed[:], sum3[:], TANH, bias=b3_sb[:])
             first_rows = squashed[:].rearrange("(q r) c i -> q r c i", r=QUAD)[:, 0, :, :]
             nc.sync.dma_start(in_quarters(out)[:, group[0] : group[-1] + 1, :], first_rows)
 
-        for c in EARLY:
+        def open_bank(chunk, h):
+            sum1[chunk, h] = psum.tile([P, PIECE], F32, name="sum1", tag="bank")
+
+        for c in WHOLE:
             for h in range(HALVES):
-                sum1[c, h] = psum.tile([P, PIECE], F32, name="sum1", tag="bank")
+                open_bank(c, h)
                 look_up(c, h, opens=True)
-        for c in EARLY:
+        for c in WHOLE:
             for h in range(HALVES):
                 add_rest(c, h, opens=False)
                 gelu1(c, h)
-        for c in EARLY:
-            layer2(c)
-        for c in LATE:
-            for h in range(HALVES):
-                sum1[c, h] = psum.tile([P, PIECE], F32, name="sum1", tag="bank")
-                add_rest(c, h, opens=True)
-        for c in LATE:
-            for h in range(HALVES):
-                look_up(c, h, opens=False)
-                gelu1(c, h)
-        for c in LATE:
-            layer2(c)
-        for group in L3_GROUPS:
-            layer3(group)
+        layer2(0)
+        layer2(1)
+        for h in range(HALVES):
+            open_bank(PART_A, h)
+            add_rest(PART_A, h, opens=True)
+        layer2(2)
+        for h in range(HALVES):
+            look_up(PART_A, h, opens=False)
+            gelu1(PART_A, h)
+        for h in range(HALVES):
+            open_bank(PART_B, h)
+            look_up(PART_B, h, opens=True)
+        for h in range(HALVES):
+            add_rest(PART_B, h, opens=False)
+            gelu1(PART_B, h)
+        layer2(PART_A)
+        layer2(PART_B)
+        sum3_whole, sum3_last = open_with_z(WHOLE), open_with_z((LAST,))
+        for k in range(HALVES):
+            add_w3(sum3_whole, h2_whole, k, range(QUARTERS))
+        squash_and_store(sum3_whole, WHOLE)
+        for chunk in (PART_A, PART_B):
+            c, a, b = CHUNKS[chunk]
+            for k in range(HALVES):
+                add_w3(sum3_last, h2_last, k, range(a // QUARTER, b // QUARTER))
+        squash_and_store(sum3_last, (LAST,))

@@ -57,11 +57,11 @@ def tile_expertpredictionheads_kernel(tc, table, w, rest, w_rest, b1, w2, b2, w3
         with nc.allow_non_contiguous_dma(reason="b1, b2, w3: 256 single elements, one to a partition and half"):
             nc.sync.dma_start(w_rest_sb[:], w_rest.rearrange("(k p) m -> p k m", p=P))
             load_rest(0)
-            nc.sync.dma_start(b1_sb[:], b1.rearrange("(h p) o -> p (h o)", p=P))
             load_rest(1)
+            nc.sync.dma_start(b1_sb[:], b1.rearrange("(h p) o -> p (h o)", p=P))
+            load_rest(2)
             nc.sync.dma_start(w2_sb[:], w2.rearrange("(k p) m -> p k m", p=P))
             nc.sync.dma_start(b2_sb[:], b2.rearrange("(h p) o -> p (h o)", p=P))
-            load_rest(2)
             load_rest(3)
             nc.sync.dma_start(w3_sb[:], w3.rearrange("(h p) o -> p (h o)", p=P))
 

import concourse.mybir as mybir
from concourse.masks import make_identity

BF16, F32, U16 = mybir.dt.bfloat16, mybir.dt.float32, mybir.dt.uint16
GELU = mybir.ActivationFunctionType.Gelu
TANH = mybir.ActivationFunctionType.Tanh
ADD, SUBTRACT = mybir.AluOpType.add, mybir.AluOpType.subtract
MIN, MAX = mybir.AluOpType.min, mybir.AluOpType.max

P = 128
S, D, R, M, N = 1024, 128, 256, 256, 2048
PIECE = 512
N_PIECES = N // PIECE
WHOLE = (0, 1, 2)
PART = PIECE // 2
LAST = N_PIECES - 1
CHUNKS = [(c, 0, PIECE) for c in WHOLE] + [(LAST, 0, PART), (LAST, PART, PIECE)]
PART_A, PART_B = len(WHOLE), len(WHOLE) + 1
HALVES = M // P
R_BLOCKS = R // P
QUAD = 32
QUARTERS = P // QUAD
QUARTER = PIECE // QUARTERS
LIST_ROWS = 16
Z_LIMIT = 3.0e38
TERM_ROWS = (0, 64, 96)
BANKS = 8

FLOPS = 2 * N * (D * M + R * M + M * M + M)


def tile_expertpredictionheads_kernel(tc, table, w, rest, w_rest, b1, w2, b2, w3, b3, z, offs, out):
    nc = tc.nc
    with (
        tc.tile_pool(name="held", bufs=1) as held,
        tc.tile_pool(name="pieces", bufs=N_PIECES) as pieces,
        tc.psum_pool(name="psum", bufs=BANKS) as psum,
    ):
        offsets = held.tile([P, N // 16], U16, name="offsets")
        nc.sync.dma_start(offsets[:], offs)
        table_sb = held.tile([P, S], BF16, name="table_sb")
        nc.sync.dma_start(table_sb[:], table)
        w_sb = held.tile([P, M], BF16, name="w_sb")
        nc.sync.dma_start(w_sb[:], w)

        b1_sb = held.tile([P, HALVES], F32, name="b1_sb")
        b2_sb = held.tile([P, HALVES], F32, name="b2_sb")
        w3_sb = held.tile([P, HALVES], BF16, name="w3_sb")
        w_rest_sb = held.tile([P, R_BLOCKS, M], BF16, name="w_rest_sb")
        w2_sb = held.tile([P, HALVES, M], BF16, name="w2_sb")
        rest_sb = [held.tile([P, R_BLOCKS, PIECE], BF16, name="rest_sb%d" % c) for c in range(N_PIECES)]
        rest_blocks = rest.rearrange("(k p) n -> p k n", p=P)

        def load_rest(c):
            nc.sync.dma_start(rest_sb[c][:], rest_blocks[:, :, c * PIECE : (c + 1) * PIECE])

        with nc.allow_non_contiguous_dma(reason="b1, b2, w3: 256 single elements, one to a partition and half"):
            nc.sync.dma_start(w_rest_sb[:], w_rest.rearrange("(k p) m -> p k m", p=P))
            load_rest(0)
            load_rest(1)
            nc.sync.dma_start(b1_sb[:], b1.rearrange("(h p) o -> p (h o)", p=P))
            load_rest(2)
            nc.sync.dma_start(w2_sb[:], w2.rearrange("(k p) m -> p k m", p=P))
            nc.sync.dma_start(b2_sb[:], b2.rearrange("(h p) o -> p (h o)", p=P))
            load_rest(3)
            nc.sync.dma_start(w3_sb[:], w3.rearrange("(h p) o -> p (h o)", p=P))

        b3_sb = held.tile([P, 1], F32, name="b3_sb")
        nc.sync.dma_start(b3_sb[:], b3.to_broadcast([P, 1]))
        def in_quarters(row):
            return row.rearrange("o (c q i) -> q (o c) i", c=N_PIECES, q=QUARTERS)

        z_copies = held.tile([P, N_PIECES, QUARTER], F32, name="z_copies")
        nc.vector.memset(z_copies[:], 0.0)
        for first in TERM_ROWS:
            nc.sync.dma_start(z_copies[first : first + QUARTERS], in_quarters(z))
        nc.vector.tensor_scalar(z_copies[:], z_copies[:], Z_LIMIT, -Z_LIMIT, MIN, MAX)
        z_terms = held.tile([P, N_PIECES, QUARTER], BF16, name="z_terms")
        nc.vector.tensor_copy(z_terms[:], z_copies[:])
        for first in TERM_ROWS[1:]:
            left = held.tile([P, N_PIECES, QUARTER], F32, name="left%d" % first)
            nc.vector.tensor_tensor(left[first:], z_copies[first:], z_terms[first:], SUBTRACT)
            nc.vector.tensor_copy(z_terms[first:], left[first:])
            z_copies = left
        identity = held.tile([P, P], BF16, name="identity")
        make_identity(nc, identity[:])
        two_terms = held.tile([P, QUARTERS], BF16, name="two_terms")
        three_terms = held.tile([P, QUARTERS], BF16, name="three_terms")
        hi, mid, lo = [identity[:, first : first + QUARTERS] for first in TERM_ROWS]
        nc.vector.tensor_tensor(two_terms[:], hi, mid, ADD)
        nc.vector.tensor_tensor(three_terms[:], two_terms[:], lo, ADD)
        sum_terms = held.tile([P, QUARTERS, QUAD], BF16, name="sum_terms")
        nc.vector.tensor_copy(sum_terms[:], three_terms[:].unsqueeze(2).to_broadcast([P, QUARTERS, QUAD]))

        w3_cols = held.tile([P, HALVES, QUAD], BF16, name="w3_cols")
        nc.vector.tensor_copy(w3_cols[:], w3_sb[:].unsqueeze(2).to_broadcast([P, HALVES, QUAD]))

        h1 = [pieces.tile([P, HALVES, PIECE], BF16, name="h1") for c in range(N_PIECES)]
        h2_whole = held.tile([P, HALVES, len(WHOLE), PIECE], BF16, name="h2_whole")
        h2_last = held.tile([P, HALVES, 1, PIECE], BF16, name="h2_last")
        sum1 = {}

        def look_up(chunk, h, opens):
            c, a, b = CHUNKS[chunk]
            first, last = (c * PIECE + a) // LIST_ROWS, (c * PIECE + b) // LIST_ROWS
            picked = table_sb[:].indirect(offsets[:, first:last])
            nc.tensor.matmul(sum1[chunk, h][:, : b - a], w_sb[:, h * P : (h + 1) * P], picked, start=opens, stop=not opens)

        def add_rest(chunk, h, opens):
            c, a, b = CHUNKS[chunk]
            for k in range(R_BLOCKS):
                nc.tensor.matmul(
                    sum1[chunk, h][:, : b - a], w_rest_sb[:, k, h * P : (h + 1) * P], rest_sb[c][:, k, a:b],
                    start=(opens and k == 0), stop=(not opens and k == R_BLOCKS - 1),
                )

        def gelu1(chunk, h):
            c, a, b = CHUNKS[chunk]
            nc.scalar.activation(h1[c][:, h, a:b], sum1[chunk, h][:, : b - a], GELU, bias=b1_sb[:, h : h + 1])

        def layer2(chunk):
            c, a, b = CHUNKS[chunk]
            for h in range(HALVES):
                sum2 = psum.tile([P, PIECE], F32, name="sum2", tag="bank")
                for k in range(HALVES):
                    nc.tensor.matmul(
                        sum2[:, : b - a], w2_sb[:, k, h * P : (h + 1) * P], h1[c][:, k, a:b],
                        start=(k == 0), stop=(k == HALVES - 1),
                    )
                h2, slot = (h2_last, 0) if c == LAST else (h2_whole, c)
                nc.scalar.activation(h2[:, h, slot, a:b], sum2[:, : b - a], GELU, bias=b2_sb[:, h : h + 1])

        def open_with_z(group):
            sum3 = psum.tile([P, len(group), QUARTER], F32, name="sum3", tag="bank")
            nc.tensor.matmul(sum3[:], sum_terms[:], z_terms[:, group[0] : group[-1] + 1, :], start=True, stop=False)
            return sum3

        def add_w3(sum3, h2, k, quarters):
            for q in quarters:
                nc.tensor.matmul(
                    sum3[q * QUAD : (q + 1) * QUAD], w3_cols[:, k, :], h2[:, k, :, q * QUARTER : (q + 1) * QUARTER],
                    start=False, stop=(k == HALVES - 1),
                )

        def squash_and_store(sum3, group):
            squashed = held.tile([P, len(group), QUARTER], F32, name="squashed%d" % group[0])
            nc.scalar.activation(squashed[:], sum3[:], TANH, bias=b3_sb[:])
            first_rows = squashed[:].rearrange("(q r) c i -> q r c i", r=QUAD)[:, 0, :, :]
            nc.sync.dma_start(in_quarters(out)[:, group[0] : group[-1] + 1, :], first_rows)

        def open_bank(chunk, h):
            sum1[chunk, h] = psum.tile([P, PIECE], F32, name="sum1", tag="bank")

        for c in WHOLE:
            for h in range(HALVES):
                open_bank(c, h)
                look_up(c, h, opens=True)
        for c in WHOLE:
            for h in range(HALVES):
                add_rest(c, h, opens=False)
                gelu1(c, h)
        layer2(0)
        layer2(1)
        for h in range(HALVES):
            open_bank(PART_A, h)
            add_rest(PART_A, h, opens=True)
        layer2(2)
        for h in range(HALVES):
            look_up(PART_A, h, opens=False)
            gelu1(PART_A, h)
        for h in range(HALVES):
            open_bank(PART_B, h)
            look_up(PART_B, h, opens=True)
        for h in range(HALVES):
            add_rest(PART_B, h, opens=False)
            gelu1(PART_B, h)
        layer2(PART_A)
        layer2(PART_B)
        sum3_whole, sum3_last = open_with_z(WHOLE), open_with_z((LAST,))
        for k in range(HALVES):
            add_w3(sum3_whole, h2_whole, k, range(QUARTERS))
        squash_and_store(sum3_whole, WHOLE)
        for chunk in (PART_A, PART_B):
            c, a, b = CHUNKS[chunk]
            for k in range(HALVES):
                add_w3(sum3_last, h2_last, k, range(a // QUARTER, b // QUARTER))
        squash_and_store(sum3_last, (LAST,))
